import numpy as np
import ml_dtypes


def mxq(x, axis, fmt="e4m3"):
    dtype, down = {"e4m3": (ml_dtypes.float8_e4m3fn, 7), "e5m2": (ml_dtypes.float8_e5m2, 14)}[fmt]
    v = np.moveaxis(np.asarray(x, np.float32).astype(ml_dtypes.bfloat16).astype(np.float64), axis, -1)
    blocks = v.reshape(v.shape[:-1] + (-1, 32))
    amax = np.abs(blocks).max(-1, keepdims=True)
    byte = np.maximum(np.where(amax > 0, np.frexp(amax)[1] - 1 + 127, 0) - down, 1)
    scale = np.exp2(byte - 127.0)
    codes = (blocks / scale).astype(np.float32).astype(dtype).astype(np.float64)
    return np.moveaxis((codes * scale).reshape(v.shape), -1, axis)


WIDE = False


def mx_kscale(k):
    if not WIDE:
        return np.ones(k)
    levels = np.array([10, -10, 5, -5, 0])
    a = np.random.permutation(np.resize(levels, k // 512 * 4)).reshape(k // 512, 4)
    idx = np.arange(k)
    return np.exp2(a[idx // 512, idx % 128 // 32])


BF16 = ml_dtypes.bfloat16


def bf(x):
    return np.asarray(x, np.float32).astype(BF16)


def f64(x):
    return np.asarray(x).astype(np.float64)


N, E, C, D1, D2 = 512, 16384, 128, 2, 2
T1 = D1 + 1


def shift_down(y, k):
    return np.pad(y, ((k, 0), (0, 0)))[:y.shape[0]] if k > 0 else y


def setup_inputs():
    s = mx_kscale(E)
    return {"x": bf(np.random.standard_normal((N, E)) * s),
            "W1": bf(np.random.standard_normal((T1, E, C)) * 0.4 / np.sqrt(E) / s[None, :, None]),
            "b1": bf(np.random.standard_normal((1, C)) * 0.25)}


def reference(x, W1, b1):
    Y = mxq(f64(x), 1, "e4m3") @ mxq(f64(W1), 1, "e4m3")
    S = sum(shift_down(Y[k], k) for k in range(T1))
    cnt1 = np.minimum(np.arange(N), D1) + 1.0
    return np.tanh(S + cnt1[:, None] * f64(b1)[0])

@@ -1,0 +1,155 @@
+from contextlib import ExitStack
+
+import concourse.mybir as mybir
+from concourse.masks import make_identity
+
+FP8X4 = mybir.dt.float8_e4m3fn_x4
+BF16 = mybir.dt.bfloat16
+F32 = mybir.dt.float32
+U32 = mybir.dt.uint32
+U8 = mybir.dt.uint8
+ACT = mybir.ActivationFunctionType
+ALU = mybir.AluOpType
+
+P = 128
+PACK = 4
+K_PASS = P * PACK
+PAIRS = PACK // 2
+
+ROWS = 512
+K = 16384
+C = 128
+TAPS = 3
+ROW_BLOCKS = ROWS // P
+
+CHUNK_PASSES = 4
+CHUNK_K = CHUNK_PASSES * K_PASS
+CHUNKS = K // CHUNK_K
+LOAD_BUFS = 4
+
+BANK_ROWS = ROWS // 2
+BANK_BLOCKS = BANK_ROWS // P
+SCALAR_TAP = TAPS - 1
+
+FLOPS = 2 * ROWS * K * C * TAPS
+
+
+def tile_predictor_pa_k_kernel(tc, x, W1, b1, out):
+    nc = tc.nc
+    with ExitStack() as pools:
+        consts = pools.enter_context(tc.tile_pool(name="consts", bufs=1))
+        loads = pools.enter_context(tc.tile_pool(name="loads", bufs=LOAD_BUFS))
+        x_stage = pools.enter_context(tc.tile_pool(name="x_stage", bufs=4))
+        w_stage = pools.enter_context(tc.tile_pool(name="w_stage", bufs=2))
+        quantised = pools.enter_context(tc.tile_pool(name="quantised", bufs=2))
+        sums = pools.enter_context(tc.psum_pool(name="sums", bufs=1))
+        turns = pools.enter_context(tc.psum_pool(name="turns", bufs=5))
+
+        ident = consts.tile([P, P], F32)
+        make_identity(nc, ident[:])
+
+        warm = consts.tile([P, 1], F32)
+        nc.vector.memset(warm[:], 0.0)
+        nc.scalar.activation(out=warm[:], in_=warm[:], func=ACT.Tanh)
+
+        bias_row = consts.tile([1, C], BF16)
+        nc.sync.dma_start(out=bias_row[:], in_=b1)
+        bias_rows = consts.tile([P, P], F32)
+        nc.vector.memset(bias_rows[:], 0.0)
+        nc.vector.tensor_copy(out=bias_rows[0:1, :], in_=bias_row[:])
+        bias_turned = turns.tile([P, PAIRS, BANK_ROWS], F32, tag="turned")
+        nc.tensor.transpose(bias_turned[:, 0, 0:P], bias_rows[:], ident[:])
+        bias = consts.tile([P, 1], F32)
+        nc.vector.tensor_copy(out=bias[:], in_=bias_turned[:, 0, 0:1])
+
+        x_by_block = x.rearrange("(r p) k -> p r k", p=P)
+        acc = [sums.tile([P, ROWS], F32, name="acc%d" % tap) for tap in range(TAPS)]
+
+        for chunk in range(CHUNKS):
+            k_rows = slice(chunk * CHUNK_K, (chunk + 1) * CHUNK_K)
+
+            x_raw = loads.tile([P, ROW_BLOCKS, CHUNK_K], BF16)
+            nc.sync.dma_start(out=x_raw[:], in_=x_by_block[:, :, k_rows])
+            w_raw = loads.tile([P, TAPS, CHUNK_PASSES, PACK * C], BF16)
+            for tap in range(TAPS):
+                nc.sync.dma_start(
+                    out=w_raw[:, tap, :, :],
+                    in_=W1[tap, k_rows, :].rearrange("(g p j) c -> p g (j c)", p=P, j=PACK),
+                )
+
+            x_codes = quantised.tile([P, CHUNK_PASSES, ROWS], U32, align_bytes=64)
+            x_scales = quantised.tile([P, CHUNK_PASSES, ROWS], U8, align_bytes=64)
+            for g in range(CHUNK_PASSES):
+                x_grouped = x_stage.tile([P, ROWS * PACK], BF16, align_bytes=64)
+                grouped_words = x_grouped[:].bitcast(F32).rearrange("p (n u) -> p n u", u=PAIRS)
+                for bank in range(ROWS // BANK_ROWS):
+                    turned = turns.tile([P, PAIRS, BANK_ROWS], F32, tag="turned")
+                    for u in range(PAIRS):
+                        for b in range(BANK_BLOCKS):
+                            words = x_raw[:, bank * BANK_BLOCKS + b, :].bitcast(F32)
+                            pass_words = words[:, g * P * PAIRS : (g + 1) * P * PAIRS]
+                            nc.tensor.transpose(
+                                turned[:, u, b * P : (b + 1) * P],
+                                pass_words[:, u : P * PAIRS : PAIRS],
+                                ident[:],
+                            )
+                    nc.scalar.copy(
+                        out=grouped_words[:, bank * BANK_ROWS : (bank + 1) * BANK_ROWS, :],
+                        in_=turned[:].rearrange("p u n -> p n u"),
+                    )
+                nc.vector.quantize_mx(
+                    out=x_codes[:, g, :].bitcast(FP8X4),
+                    scales=x_scales[:, g, :],
+                    in_=x_grouped[:],
+                )
+
+            w_grouped = w_stage.tile([P, TAPS, CHUNK_PASSES * C * PACK], BF16, align_bytes=64)
+            w_codes = quantised.tile([P, TAPS, CHUNK_PASSES * C], U32, align_bytes=64)
+            w_scales = quantised.tile([P, TAPS, CHUNK_PASSES * C], U8, align_bytes=64)
+            for tap in range(TAPS):
+                side_by_side = w_grouped[:, tap, :].rearrange("p (g c j) -> p g c j", c=C, j=PACK)
+                rows_apart = w_raw[:, tap, :, :].rearrange("p g (j c) -> p g c j", j=PACK)
+                if tap == SCALAR_TAP:
+                    nc.scalar.copy(out=side_by_side, in_=rows_apart)
+                else:
+                    nc.vector.tensor_copy(out=side_by_side, in_=rows_apart)
+            for tap in range(TAPS):
+                nc.vector.quantize_mx(
+                    out=w_codes[:, tap, :].bitcast(FP8X4),
+                    scales=w_scales[:, tap, :],
+                    in_=w_grouped[:, tap, :],
+                )
+
+            for tap in range(TAPS):
+                for g in range(CHUNK_PASSES):
+                    channels = slice(g * C, (g + 1) * C)
+                    nc.tensor.matmul_mx(
+                        out=acc[tap][:],
+                        lhsT=w_codes[:, tap, channels].bitcast(FP8X4),
+                        lhsT_scale=w_scales[:, tap, channels],
+                        rhs=x_codes[:, g, :].bitcast(FP8X4),
+                        rhs_scale=x_scales[:, g, :],
+                        start=(chunk == 0 and g == 0),
+                        stop=(chunk == CHUNKS - 1 and g == CHUNK_PASSES - 1),
+                    )
+
+        shifted = consts.tile([P, ROWS], F32)
+        nc.vector.tensor_scalar(
+            out=shifted[:], in0=acc[0][:], scalar1=bias[:, 0:1], scalar2=None, op0=ALU.add
+        )
+        for tap in range(1, TAPS):
+            nc.vector.scalar_tensor_tensor(
+                out=shifted[:, tap:ROWS],
+                in0=acc[tap][:, 0 : ROWS - tap],
+                scalar=bias[:, 0:1],
+                in1=shifted[:, tap:ROWS],
+                op0=ALU.add,
+                op1=ALU.add,
+            )
+
+        result_turned = turns.tile([P, ROW_BLOCKS, C], F32, tag="turned")
+        for r in range(ROW_BLOCKS):
+            nc.tensor.transpose(result_turned[:, r, :], shifted[:, r * P : (r + 1) * P], ident[:])
+        result = consts.tile([P, ROW_BLOCKS, C], F32)
+        nc.scalar.activation(out=result[:], in_=result_turned[:], func=ACT.Tanh)
+        nc.sync.dma_start(out=out.rearrange("(r p) c -> p r c", p=P), in_=result[:])

@@ -73,8 +73,8 @@ def tile_predictor_pa_k_kernel(tc, x, W1, b1, out):
             w_raw = loads.tile([P, TAPS, CHUNK_PASSES, PACK * C], BF16)
             for tap in range(TAPS):
                 nc.sync.dma_start(
-                    out=w_raw[:, tap, :, :],
-                    in_=W1[tap, k_rows, :].rearrange("(g p j) c -> p g (j c)", p=P, j=PACK),
+                    out=w_raw[:, tap, :, :].rearrange("p g (u f) -> p (g u) f", u=PAIRS),
+                    in_=W1[tap, k_rows, :].rearrange("(s p e) c -> p s (e c)", p=P, e=2),
                 )
 
             x_codes = quantised.tile([P, CHUNK_PASSES, ROWS], U32, align_bytes=64)
@@ -90,7 +90,7 @@ def tile_predictor_pa_k_kernel(tc, x, W1, b1, out):
                             pass_words = words[:, g * P * PAIRS : (g + 1) * P * PAIRS]
                             nc.tensor.transpose(
                                 turned[:, u, b * P : (b + 1) * P],
-                                pass_words[:, u : P * PAIRS : PAIRS],
+                                pass_words[:, u * P : (u + 1) * P],
                                 ident[:],
                             )
                     nc.scalar.copy(

@@ -15,6 +15,7 @@ P = 128
 PACK = 4
 K_PASS = P * PACK
 PAIRS = PACK // 2
+PASS_WORDS = K_PASS // 2
 
 ROWS = 512
 K = 16384
@@ -22,13 +23,17 @@ C = 128
 TAPS = 3
 ROW_BLOCKS = ROWS // P
 
-CHUNK_PASSES = 4
+ROUND_PASSES = 2
+ROUNDS = K // (ROUND_PASSES * K_PASS)
+CHUNK_ROUNDS = 2
+CHUNK_PASSES = CHUNK_ROUNDS * ROUND_PASSES
 CHUNK_K = CHUNK_PASSES * K_PASS
 CHUNKS = K // CHUNK_K
 LOAD_BUFS = 4
 
 BANK_ROWS = ROWS // 2
 BANK_BLOCKS = BANK_ROWS // P
+PASS_BANKS = ROWS // BANK_ROWS
 SCALAR_TAP = TAPS - 1
 
 FLOPS = 2 * ROWS * K * C * TAPS
@@ -39,9 +44,9 @@ def tile_predictor_pa_k_kernel(tc, x, W1, b1, out):
     with ExitStack() as pools:
         consts = pools.enter_context(tc.tile_pool(name="consts", bufs=1))
         loads = pools.enter_context(tc.tile_pool(name="loads", bufs=LOAD_BUFS))
-        x_stage = pools.enter_context(tc.tile_pool(name="x_stage", bufs=4))
+        x_stage = pools.enter_context(tc.tile_pool(name="x_stage", bufs=2 * ROUND_PASSES))
         w_stage = pools.enter_context(tc.tile_pool(name="w_stage", bufs=2))
-        quantised = pools.enter_context(tc.tile_pool(name="quantised", bufs=2))
+        quantised = pools.enter_context(tc.tile_pool(name="quantised", bufs=3))
         sums = pools.enter_context(tc.psum_pool(name="sums", bufs=1))
         turns = pools.enter_context(tc.psum_pool(name="turns", bufs=5))
 
@@ -64,92 +69,132 @@ def tile_predictor_pa_k_kernel(tc, x, W1, b1, out):
 
         x_by_block = x.rearrange("(r p) k -> p r k", p=P)
         acc = [sums.tile([P, ROWS], F32, name="acc%d" % tap) for tap in range(TAPS)]
+        x_raw = {}
+        w_raw = {}
+        x_grouped = {}
+        w_grouped = {}
+        x_codes, x_scales, w_codes, w_scales = {}, {}, {}, {}
 
-        for chunk in range(CHUNKS):
+        def load_chunk(chunk):
             k_rows = slice(chunk * CHUNK_K, (chunk + 1) * CHUNK_K)
-
-            x_raw = loads.tile([P, ROW_BLOCKS, CHUNK_K], BF16)
-            nc.sync.dma_start(out=x_raw[:], in_=x_by_block[:, :, k_rows])
-            w_raw = loads.tile([P, TAPS, CHUNK_PASSES, PACK * C], BF16)
+            x_raw[chunk] = loads.tile([P, ROW_BLOCKS, CHUNK_K], BF16, name="x_raw")
+            nc.sync.dma_start(out=x_raw[chunk][:], in_=x_by_block[:, :, k_rows])
+            w_raw[chunk] = loads.tile([P, TAPS, CHUNK_PASSES, PACK * C], BF16, name="w_raw")
             for tap in range(TAPS):
                 nc.sync.dma_start(
-                    out=w_raw[:, tap, :, :].rearrange("p g (u f) -> p (g u) f", u=PAIRS),
-                    in_=W1[tap, k_rows, :].rearrange("(s p e) c -> p s (e c)", p=P, e=2),
+                    out=w_raw[chunk][:, tap, :, :],
+                    in_=W1[tap, k_rows, :].rearrange("(g p j) c -> p g (j c)", p=P, j=PACK),
                 )
 
-            x_codes = quantised.tile([P, CHUNK_PASSES, ROWS], U32, align_bytes=64)
-            x_scales = quantised.tile([P, CHUNK_PASSES, ROWS], U8, align_bytes=64)
-            for g in range(CHUNK_PASSES):
-                x_grouped = x_stage.tile([P, ROWS * PACK], BF16, align_bytes=64)
-                grouped_words = x_grouped[:].bitcast(F32).rearrange("p (n u) -> p n u", u=PAIRS)
-                for bank in range(ROWS // BANK_ROWS):
+        def turn_x(rnd):
+            raw = x_raw[rnd // CHUNK_ROUNDS]
+            x_grouped[rnd] = []
+            for g in range(ROUND_PASSES):
+                first_word = ((rnd % CHUNK_ROUNDS) * ROUND_PASSES + g) * PASS_WORDS
+                grouped = x_stage.tile([P, ROWS * PACK], BF16, align_bytes=64, name="x_grouped")
+                x_grouped[rnd].append(grouped)
+                grouped_words = grouped[:].bitcast(F32).rearrange("p (n u) -> p n u", u=PAIRS)
+                for bank in range(PASS_BANKS):
                     turned = turns.tile([P, PAIRS, BANK_ROWS], F32, tag="turned")
                     for u in range(PAIRS):
                         for b in range(BANK_BLOCKS):
-                            words = x_raw[:, bank * BANK_BLOCKS + b, :].bitcast(F32)
-                            pass_words = words[:, g * P * PAIRS : (g + 1) * P * PAIRS]
+                            words = raw[:, bank * BANK_BLOCKS + b, :].bitcast(F32)
                             nc.tensor.transpose(
                                 turned[:, u, b * P : (b + 1) * P],
-                                pass_words[:, u * P : (u + 1) * P],
+                                words[:, first_word + u : first_word + PASS_WORDS : PAIRS],
                                 ident[:],
                             )
                     nc.scalar.copy(
                         out=grouped_words[:, bank * BANK_ROWS : (bank + 1) * BANK_ROWS, :],
                         in_=turned[:].rearrange("p u n -> p n u"),
                     )
-                nc.vector.quantize_mx(
-                    out=x_codes[:, g, :].bitcast(FP8X4),
-                    scales=x_scales[:, g, :],
-                    in_=x_grouped[:],
-                )
 
-            w_grouped = w_stage.tile([P, TAPS, CHUNK_PASSES * C * PACK], BF16, align_bytes=64)
-            w_codes = quantised.tile([P, TAPS, CHUNK_PASSES * C], U32, align_bytes=64)
-            w_scales = quantised.tile([P, TAPS, CHUNK_PASSES * C], U8, align_bytes=64)
+        def regroup_w(rnd):
+            raw = w_raw[rnd // CHUNK_ROUNDS]
+            first_pass = (rnd % CHUNK_ROUNDS) * ROUND_PASSES
+            w_grouped[rnd] = w_stage.tile(
+                [P, TAPS, ROUND_PASSES * C * PACK], BF16, align_bytes=64, name="w_grouped"
+            )
             for tap in range(TAPS):
-                side_by_side = w_grouped[:, tap, :].rearrange("p (g c j) -> p g c j", c=C, j=PACK)
-                rows_apart = w_raw[:, tap, :, :].rearrange("p g (j c) -> p g c j", j=PACK)
+                side_by_side = w_grouped[rnd][:, tap, :].rearrange(
+                    "p (g c j) -> p g c j", c=C, j=PACK
+                )
+                rows_apart = raw[:, tap, first_pass : first_pass + ROUND_PASSES, :].rearrange(
+                    "p g (j c) -> p g c j", j=PACK
+                )
                 if tap == SCALAR_TAP:
                     nc.scalar.copy(out=side_by_side, in_=rows_apart)
                 else:
                     nc.vector.tensor_copy(out=side_by_side, in_=rows_apart)
-            for tap in range(TAPS):
+
+        def quantise_x(rnd):
+            x_codes[rnd] = quantised.tile([P, ROUND_PASSES, ROWS], U32, align_bytes=64, name="x_codes")
+            x_scales[rnd] = quantised.tile([P, ROUND_PASSES, ROWS], U8, align_bytes=64, name="x_scales")
+            for g in range(ROUND_PASSES):
                 nc.vector.quantize_mx(
-                    out=w_codes[:, tap, :].bitcast(FP8X4),
-                    scales=w_scales[:, tap, :],
-                    in_=w_grouped[:, tap, :],
+                    out=x_codes[rnd][:, g, :].bitcast(FP8X4),
+                    scales=x_scales[rnd][:, g, :],
+                    in_=x_grouped[rnd][g][:],
                 )
 
+        def quantise_w(rnd):
+            w_codes[rnd] = quantised.tile([P, TAPS, ROUND_PASSES * C], U32, align_bytes=64, name="w_codes")
+            w_scales[rnd] = quantised.tile([P, TAPS, ROUND_PASSES * C], U8, align_bytes=64, name="w_scales")
             for tap in range(TAPS):
-                for g in range(CHUNK_PASSES):
+                nc.vector.quantize_mx(
+                    out=w_codes[rnd][:, tap, :].bitcast(FP8X4),
+                    scales=w_scales[rnd][:, tap, :],
+                    in_=w_grouped[rnd][:, tap, :],
+                )
+
+        def multiply(rnd):
+            for tap in range(TAPS):
+                for g in range(ROUND_PASSES):
                     channels = slice(g * C, (g + 1) * C)
                     nc.tensor.matmul_mx(
                         out=acc[tap][:],
-                        lhsT=w_codes[:, tap, channels].bitcast(FP8X4),
-                        lhsT_scale=w_scales[:, tap, channels],
-                        rhs=x_codes[:, g, :].bitcast(FP8X4),
-                        rhs_scale=x_scales[:, g, :],
-                        start=(chunk == 0 and g == 0),
-                        stop=(chunk == CHUNKS - 1 and g == CHUNK_PASSES - 1),
+                        lhsT=w_codes[rnd][:, tap, channels].bitcast(FP8X4),
+                        lhsT_scale=w_scales[rnd][:, tap, channels],
+                        rhs=x_codes[rnd][:, g, :].bitcast(FP8X4),
+                        rhs_scale=x_scales[rnd][:, g, :],
+                        start=(rnd == 0 and g == 0),
+                        stop=(rnd == ROUNDS - 1 and g == ROUND_PASSES - 1),
                     )
 
-        shifted = consts.tile([P, ROWS], F32)
-        nc.vector.tensor_scalar(
-            out=shifted[:], in0=acc[0][:], scalar1=bias[:, 0:1], scalar2=None, op0=ALU.add
-        )
-        for tap in range(1, TAPS):
-            nc.vector.scalar_tensor_tensor(
-                out=shifted[:, tap:ROWS],
-                in0=acc[tap][:, 0 : ROWS - tap],
-                scalar=bias[:, 0:1],
-                in1=shifted[:, tap:ROWS],
-                op0=ALU.add,
-                op1=ALU.add,
-            )
+        with tc.manual_schedule():
+            for chunk in range(LOAD_BUFS):
+                load_chunk(chunk)
+            for rnd in range(ROUNDS + 1):
+                if rnd < ROUNDS:
+                    turn_x(rnd)
+                    regroup_w(rnd)
+                    quantise_x(rnd)
+                    quantise_w(rnd)
+                    next_chunk = rnd // CHUNK_ROUNDS + LOAD_BUFS
+                    if rnd % CHUNK_ROUNDS == CHUNK_ROUNDS - 1 and next_chunk < CHUNKS:
+                        load_chunk(next_chunk)
+                if rnd > 0:
+                    multiply(rnd - 1)
 
-        result_turned = turns.tile([P, ROW_BLOCKS, C], F32, tag="turned")
-        for r in range(ROW_BLOCKS):
-            nc.tensor.transpose(result_turned[:, r, :], shifted[:, r * P : (r + 1) * P], ident[:])
-        result = consts.tile([P, ROW_BLOCKS, C], F32)
-        nc.scalar.activation(out=result[:], in_=result_turned[:], func=ACT.Tanh)
-        nc.sync.dma_start(out=out.rearrange("(r p) c -> p r c", p=P), in_=result[:])
+            shifted = consts.tile([P, ROWS], F32)
+            nc.vector.tensor_scalar(
+                out=shifted[:], in0=acc[0][:], scalar1=bias[:, 0:1], scalar2=None, op0=ALU.add
+            )
+            for tap in range(1, TAPS):
+                nc.vector.scalar_tensor_tensor(
+                    out=shifted[:, tap:ROWS],
+                    in0=acc[tap][:, 0 : ROWS - tap],
+                    scalar=bias[:, 0:1],
+                    in1=shifted[:, tap:ROWS],
+                    op0=ALU.add,
+                    op1=ALU.add,
+                )
+
+            result_turned = turns.tile([P, ROW_BLOCKS, C], F32, tag="turned")
+            for r in range(ROW_BLOCKS):
+                nc.tensor.transpose(
+                    result_turned[:, r, :], shifted[:, r * P : (r + 1) * P], ident[:]
+                )
+            result = consts.tile([P, ROW_BLOCKS, C], F32)
+            nc.scalar.activation(out=result[:], in_=result_turned[:], func=ACT.Tanh)
+            nc.sync.dma_start(out=out.rearrange("(r p) c -> p r c", p=P), in_=result[:])

@@ -22,19 +22,24 @@ K = 16384
 C = 128
 TAPS = 3
 ROW_BLOCKS = ROWS // P
+PASSES = K // K_PASS
 
-ROUND_PASSES = 2
-ROUNDS = K // (ROUND_PASSES * K_PASS)
-CHUNK_ROUNDS = 2
-CHUNK_PASSES = CHUNK_ROUNDS * ROUND_PASSES
-CHUNK_K = CHUNK_PASSES * K_PASS
-CHUNKS = K // CHUNK_K
-LOAD_BUFS = 4
-
-BANK_ROWS = ROWS // 2
+BANK_ROWS = 256
 BANK_BLOCKS = BANK_ROWS // P
-PASS_BANKS = ROWS // BANK_ROWS
-SCALAR_TAP = TAPS - 1
+ROW_HALVES = ROWS // BANK_ROWS
+X_LOAD_PASSES = 8
+X_LOAD_K = X_LOAD_PASSES * K_PASS
+X_LOADS = ROW_HALVES * K // X_LOAD_K
+X_BANKS = X_LOADS * X_LOAD_PASSES
+X_BUFS = 4
+VECTOR_EVERY = 4
+
+PIECE_PASSES = 4
+PIECE_K = PIECE_PASSES * K_PASS
+PIECES = TAPS * K // PIECE_K
+W_BUFS = 8
+VECTOR_PASSES = PIECE_PASSES // 2
+RUN = 4
 
 FLOPS = 2 * ROWS * K * C * TAPS
 
@@ -43,10 +48,10 @@ def tile_predictor_pa_k_kernel(tc, x, W1, b1, out):
     nc = tc.nc
     with ExitStack() as pools:
         consts = pools.enter_context(tc.tile_pool(name="consts", bufs=1))
-        loads = pools.enter_context(tc.tile_pool(name="loads", bufs=LOAD_BUFS))
-        x_stage = pools.enter_context(tc.tile_pool(name="x_stage", bufs=2 * ROUND_PASSES))
-        w_stage = pools.enter_context(tc.tile_pool(name="w_stage", bufs=2))
-        quantised = pools.enter_context(tc.tile_pool(name="quantised", bufs=3))
+        x_loads = pools.enter_context(tc.tile_pool(name="x_loads", bufs=X_BUFS))
+        x_stage = pools.enter_context(tc.tile_pool(name="x_stage", bufs=6))
+        w_loads = pools.enter_context(tc.tile_pool(name="w_loads", bufs=W_BUFS))
+        w_stage = pools.enter_context(tc.tile_pool(name="w_stage", bufs=3))
         sums = pools.enter_context(tc.psum_pool(name="sums", bufs=1))
         turns = pools.enter_context(tc.psum_pool(name="turns", bufs=5))
 
@@ -67,114 +72,119 @@ def tile_predictor_pa_k_kernel(tc, x, W1, b1, out):
         bias = consts.tile([P, 1], F32)
         nc.vector.tensor_copy(out=bias[:], in_=bias_turned[:, 0, 0:1])
 
-        x_by_block = x.rearrange("(r p) k -> p r k", p=P)
+        x_by_half = x.rearrange("(h b p) k -> h p b k", b=BANK_BLOCKS, p=P)
+        x_codes = consts.tile([P, PASSES, ROWS], U32, align_bytes=64)
+        x_scales = consts.tile([P, PASSES, ROWS], U8, align_bytes=64)
         acc = [sums.tile([P, ROWS], F32, name="acc%d" % tap) for tap in range(TAPS)]
         x_raw = {}
-        w_raw = {}
         x_grouped = {}
-        w_grouped = {}
-        x_codes, x_scales, w_codes, w_scales = {}, {}, {}, {}
+        w_raw, w_grouped, w_codes, w_scales = {}, {}, {}, {}
 
-        def load_chunk(chunk):
-            k_rows = slice(chunk * CHUNK_K, (chunk + 1) * CHUNK_K)
-            x_raw[chunk] = loads.tile([P, ROW_BLOCKS, CHUNK_K], BF16, name="x_raw")
-            nc.sync.dma_start(out=x_raw[chunk][:], in_=x_by_block[:, :, k_rows])
-            w_raw[chunk] = loads.tile([P, TAPS, CHUNK_PASSES, PACK * C], BF16, name="w_raw")
-            for tap in range(TAPS):
-                nc.sync.dma_start(
-                    out=w_raw[chunk][:, tap, :, :],
-                    in_=W1[tap, k_rows, :].rearrange("(g p j) c -> p g (j c)", p=P, j=PACK),
-                )
-
-        def turn_x(rnd):
-            raw = x_raw[rnd // CHUNK_ROUNDS]
-            x_grouped[rnd] = []
-            for g in range(ROUND_PASSES):
-                first_word = ((rnd % CHUNK_ROUNDS) * ROUND_PASSES + g) * PASS_WORDS
-                grouped = x_stage.tile([P, ROWS * PACK], BF16, align_bytes=64, name="x_grouped")
-                x_grouped[rnd].append(grouped)
-                grouped_words = grouped[:].bitcast(F32).rearrange("p (n u) -> p n u", u=PAIRS)
-                for bank in range(PASS_BANKS):
-                    turned = turns.tile([P, PAIRS, BANK_ROWS], F32, tag="turned")
-                    for u in range(PAIRS):
-                        for b in range(BANK_BLOCKS):
-                            words = raw[:, bank * BANK_BLOCKS + b, :].bitcast(F32)
-                            nc.tensor.transpose(
-                                turned[:, u, b * P : (b + 1) * P],
-                                words[:, first_word + u : first_word + PASS_WORDS : PAIRS],
-                                ident[:],
-                            )
-                    nc.scalar.copy(
-                        out=grouped_words[:, bank * BANK_ROWS : (bank + 1) * BANK_ROWS, :],
-                        in_=turned[:].rearrange("p u n -> p n u"),
-                    )
-
-        def regroup_w(rnd):
-            raw = w_raw[rnd // CHUNK_ROUNDS]
-            first_pass = (rnd % CHUNK_ROUNDS) * ROUND_PASSES
-            w_grouped[rnd] = w_stage.tile(
-                [P, TAPS, ROUND_PASSES * C * PACK], BF16, align_bytes=64, name="w_grouped"
+        def load_x(load):
+            part, half = divmod(load, ROW_HALVES)
+            x_raw[load] = x_loads.tile([P, BANK_BLOCKS, X_LOAD_K], BF16, name="x_raw")
+            nc.sync.dma_start(
+                out=x_raw[load][:],
+                in_=x_by_half[half, :, :, part * X_LOAD_K : (part + 1) * X_LOAD_K],
             )
-            for tap in range(TAPS):
-                side_by_side = w_grouped[rnd][:, tap, :].rearrange(
-                    "p (g c j) -> p g c j", c=C, j=PACK
-                )
-                rows_apart = raw[:, tap, first_pass : first_pass + ROUND_PASSES, :].rearrange(
-                    "p g (j c) -> p g c j", j=PACK
-                )
-                if tap == SCALAR_TAP:
-                    nc.scalar.copy(out=side_by_side, in_=rows_apart)
-                else:
-                    nc.vector.tensor_copy(out=side_by_side, in_=rows_apart)
 
-        def quantise_x(rnd):
-            x_codes[rnd] = quantised.tile([P, ROUND_PASSES, ROWS], U32, align_bytes=64, name="x_codes")
-            x_scales[rnd] = quantised.tile([P, ROUND_PASSES, ROWS], U8, align_bytes=64, name="x_scales")
-            for g in range(ROUND_PASSES):
-                nc.vector.quantize_mx(
-                    out=x_codes[rnd][:, g, :].bitcast(FP8X4),
-                    scales=x_scales[rnd][:, g, :],
-                    in_=x_grouped[rnd][g][:],
-                )
-
-        def quantise_w(rnd):
-            w_codes[rnd] = quantised.tile([P, TAPS, ROUND_PASSES * C], U32, align_bytes=64, name="w_codes")
-            w_scales[rnd] = quantised.tile([P, TAPS, ROUND_PASSES * C], U8, align_bytes=64, name="w_scales")
-            for tap in range(TAPS):
-                nc.vector.quantize_mx(
-                    out=w_codes[rnd][:, tap, :].bitcast(FP8X4),
-                    scales=w_scales[rnd][:, tap, :],
-                    in_=w_grouped[rnd][:, tap, :],
-                )
-
-        def multiply(rnd):
-            for tap in range(TAPS):
-                for g in range(ROUND_PASSES):
-                    channels = slice(g * C, (g + 1) * C)
-                    nc.tensor.matmul_mx(
-                        out=acc[tap][:],
-                        lhsT=w_codes[rnd][:, tap, channels].bitcast(FP8X4),
-                        lhsT_scale=w_scales[rnd][:, tap, channels],
-                        rhs=x_codes[rnd][:, g, :].bitcast(FP8X4),
-                        rhs_scale=x_scales[rnd][:, g, :],
-                        start=(rnd == 0 and g == 0),
-                        stop=(rnd == ROUNDS - 1 and g == ROUND_PASSES - 1),
+        def turn_bank(bank):
+            load, g = divmod(bank, X_LOAD_PASSES)
+            turned = turns.tile([P, PAIRS, BANK_ROWS], F32, tag="turned")
+            for u in range(PAIRS):
+                for b in range(BANK_BLOCKS):
+                    words = x_raw[load][:, b, :].bitcast(F32)
+                    nc.tensor.transpose(
+                        turned[:, u, b * P : (b + 1) * P],
+                        words[:, g * PASS_WORDS + u : (g + 1) * PASS_WORDS : PAIRS],
+                        ident[:],
                     )
+            x_grouped[bank] = x_stage.tile([P, BANK_ROWS * PACK], BF16, align_bytes=64, name="x_grouped")
+            grouped_words = x_grouped[bank][:].bitcast(F32).rearrange("p (n u) -> p n u", u=PAIRS)
+            planes_alternately = turned[:].rearrange("p u n -> p n u")
+            if bank % VECTOR_EVERY == VECTOR_EVERY - 1:
+                nc.vector.tensor_copy(out=grouped_words, in_=planes_alternately)
+            else:
+                nc.scalar.copy(out=grouped_words, in_=planes_alternately)
+
+        def quantise_bank(bank):
+            load, g = divmod(bank, X_LOAD_PASSES)
+            part, half = divmod(load, ROW_HALVES)
+            sentences = slice(half * BANK_ROWS, (half + 1) * BANK_ROWS)
+            nc.vector.quantize_mx(
+                out=x_codes[:, part * X_LOAD_PASSES + g, sentences].bitcast(FP8X4),
+                scales=x_scales[:, part * X_LOAD_PASSES + g, sentences],
+                in_=x_grouped[bank][:],
+            )
+
+        def load_w(piece):
+            part, tap = divmod(piece, TAPS)
+            w_raw[piece] = w_loads.tile([P, PIECE_PASSES, PACK * C], BF16, name="w_raw")
+            nc.sync.dma_start(
+                out=w_raw[piece][:],
+                in_=W1[tap, part * PIECE_K : (part + 1) * PIECE_K, :].rearrange(
+                    "(g p j) c -> p g (j c)", p=P, j=PACK
+                ),
+            )
+
+        def regroup_w(piece):
+            w_grouped[piece] = w_stage.tile(
+                [P, PIECE_PASSES, C * PACK], BF16, align_bytes=64, name="w_grouped"
+            )
+            side_by_side = w_grouped[piece][:].rearrange("p g (c i j) -> p g c j i", i=RUN, j=PACK)
+            rows_apart = w_raw[piece][:].rearrange("p g (j c i) -> p g c j i", j=PACK, i=RUN)
+            nc.vector.tensor_copy(
+                out=side_by_side[:, 0:VECTOR_PASSES], in_=rows_apart[:, 0:VECTOR_PASSES]
+            )
+            for g in range(VECTOR_PASSES, PIECE_PASSES):
+                nc.scalar.copy(out=side_by_side[:, g], in_=rows_apart[:, g])
+
+        def quantise_w(piece):
+            w_codes[piece] = w_stage.tile([P, PIECE_PASSES * C], U32, align_bytes=64, name="w_codes")
+            w_scales[piece] = w_stage.tile([P, PIECE_PASSES * C], U8, align_bytes=64, name="w_scales")
+            nc.vector.quantize_mx(
+                out=w_codes[piece][:].bitcast(FP8X4),
+                scales=w_scales[piece][:],
+                in_=w_grouped[piece][:].rearrange("p g f -> p (g f)"),
+            )
+
+        def multiply(piece):
+            part, tap = divmod(piece, TAPS)
+            for g in range(PIECE_PASSES):
+                pass_index = part * PIECE_PASSES + g
+                channels = slice(g * C, (g + 1) * C)
+                nc.tensor.matmul_mx(
+                    out=acc[tap][:],
+                    lhsT=w_codes[piece][:, channels].bitcast(FP8X4),
+                    lhsT_scale=w_scales[piece][:, channels],
+                    rhs=x_codes[:, pass_index, :].bitcast(FP8X4),
+                    rhs_scale=x_scales[:, pass_index, :],
+                    start=(pass_index == 0),
+                    stop=(pass_index == PASSES - 1),
+                )
 
         with tc.manual_schedule():
-            for chunk in range(LOAD_BUFS):
-                load_chunk(chunk)
-            for rnd in range(ROUNDS + 1):
-                if rnd < ROUNDS:
-                    turn_x(rnd)
-                    regroup_w(rnd)
-                    quantise_x(rnd)
-                    quantise_w(rnd)
-                    next_chunk = rnd // CHUNK_ROUNDS + LOAD_BUFS
-                    if rnd % CHUNK_ROUNDS == CHUNK_ROUNDS - 1 and next_chunk < CHUNKS:
-                        load_chunk(next_chunk)
-                if rnd > 0:
-                    multiply(rnd - 1)
+            for load in range(X_BUFS):
+                load_x(load)
+            for bank in range(X_BANKS + 1):
+                if bank < X_BANKS:
+                    turn_bank(bank)
+                    next_load = bank // X_LOAD_PASSES + X_BUFS
+                    if bank % X_LOAD_PASSES == X_LOAD_PASSES - 1 and next_load < X_LOADS:
+                        load_x(next_load)
+                if bank > 0:
+                    quantise_bank(bank - 1)
+
+            for piece in range(W_BUFS):
+                load_w(piece)
+            for piece in range(PIECES + 1):
+                if piece < PIECES:
+                    regroup_w(piece)
+                    if piece + W_BUFS < PIECES:
+                        load_w(piece + W_BUFS)
+                if piece > 0:
+                    quantise_w(piece - 1)
+                    multiply(piece - 1)
 
             shifted = consts.tile([P, ROWS], F32)
             nc.vector.tensor_scalar(

@@ -24,21 +24,26 @@ TAPS = 3
 ROW_BLOCKS = ROWS // P
 PASSES = K // K_PASS
 
-BANK_ROWS = 256
-BANK_BLOCKS = BANK_ROWS // P
-ROW_HALVES = ROWS // BANK_ROWS
+BANK_PASSES = 2
 X_LOAD_PASSES = 8
 X_LOAD_K = X_LOAD_PASSES * K_PASS
-X_LOADS = ROW_HALVES * K // X_LOAD_K
-X_BANKS = X_LOADS * X_LOAD_PASSES
-X_BUFS = 4
-VECTOR_EVERY = 4
+X_LOAD_BANKS = X_LOAD_PASSES // BANK_PASSES
+X_LOADS = ROW_BLOCKS * K // X_LOAD_K
+X_BUFS = 8
+HALF_BLOCKS = 2
+HALF_ROWS = HALF_BLOCKS * P
 
-PIECE_PASSES = 4
-PIECE_K = PIECE_PASSES * K_PASS
-PIECES = TAPS * K // PIECE_K
+PART_PASSES = 4
+SHORT_PASSES = PART_PASSES // 2
+WHOLE_PIECES = [
+    (tap, part * PART_PASSES, PART_PASSES) for part in range(PASSES // PART_PASSES) for tap in range(TAPS)
+]
+PIECES = WHOLE_PIECES[:-1] + [
+    (TAPS - 1, PASSES - 2 * SHORT_PASSES, SHORT_PASSES),
+    (TAPS - 1, PASSES - SHORT_PASSES, SHORT_PASSES),
+]
 W_BUFS = 8
-VECTOR_PASSES = PIECE_PASSES // 2
+HEAD_PIECES = 2
 RUN = 4
 
 FLOPS = 2 * ROWS * K * C * TAPS
@@ -49,9 +54,10 @@ def tile_predictor_pa_k_kernel(tc, x, W1, b1, out):
     with ExitStack() as pools:
         consts = pools.enter_context(tc.tile_pool(name="consts", bufs=1))
         x_loads = pools.enter_context(tc.tile_pool(name="x_loads", bufs=X_BUFS))
-        x_stage = pools.enter_context(tc.tile_pool(name="x_stage", bufs=6))
+        x_stage = pools.enter_context(tc.tile_pool(name="x_stage", bufs=7))
         w_loads = pools.enter_context(tc.tile_pool(name="w_loads", bufs=W_BUFS))
         w_stage = pools.enter_context(tc.tile_pool(name="w_stage", bufs=3))
+        w_quantised = pools.enter_context(tc.tile_pool(name="w_quantised", bufs=HEAD_PIECES + 2))
         sums = pools.enter_context(tc.psum_pool(name="sums", bufs=1))
         turns = pools.enter_context(tc.psum_pool(name="turns", bufs=5))
 
@@ -67,12 +73,11 @@ def tile_predictor_pa_k_kernel(tc, x, W1, b1, out):
         bias_rows = consts.tile([P, P], F32)
         nc.vector.memset(bias_rows[:], 0.0)
         nc.vector.tensor_copy(out=bias_rows[0:1, :], in_=bias_row[:])
-        bias_turned = turns.tile([P, PAIRS, BANK_ROWS], F32, tag="turned")
-        nc.tensor.transpose(bias_turned[:, 0, 0:P], bias_rows[:], ident[:])
+        bias_turned = turns.tile([P, P], F32, tag="turned")
+        nc.tensor.transpose(bias_turned[:], bias_rows[:], ident[:])
         bias = consts.tile([P, 1], F32)
-        nc.vector.tensor_copy(out=bias[:], in_=bias_turned[:, 0, 0:1])
+        nc.vector.tensor_copy(out=bias[:], in_=bias_turned[:, 0:1])
 
-        x_by_half = x.rearrange("(h b p) k -> h p b k", b=BANK_BLOCKS, p=P)
         x_codes = consts.tile([P, PASSES, ROWS], U32, align_bytes=64)
         x_scales = consts.tile([P, PASSES, ROWS], U8, align_bytes=64)
         acc = [sums.tile([P, ROWS], F32, name="acc%d" % tap) for tap in range(TAPS)]
@@ -81,67 +86,74 @@ def tile_predictor_pa_k_kernel(tc, x, W1, b1, out):
         w_raw, w_grouped, w_codes, w_scales = {}, {}, {}, {}
 
         def load_x(load):
-            part, half = divmod(load, ROW_HALVES)
-            x_raw[load] = x_loads.tile([P, BANK_BLOCKS, X_LOAD_K], BF16, name="x_raw")
+            part, block = divmod(load, ROW_BLOCKS)
+            x_raw[load] = x_loads.tile([P, X_LOAD_K], BF16, name="x_raw")
             nc.sync.dma_start(
                 out=x_raw[load][:],
-                in_=x_by_half[half, :, :, part * X_LOAD_K : (part + 1) * X_LOAD_K],
+                in_=x[block * P : (block + 1) * P, part * X_LOAD_K : (part + 1) * X_LOAD_K],
             )
 
-        def turn_bank(bank):
-            load, g = divmod(bank, X_LOAD_PASSES)
-            turned = turns.tile([P, PAIRS, BANK_ROWS], F32, tag="turned")
-            for u in range(PAIRS):
-                for b in range(BANK_BLOCKS):
-                    words = x_raw[load][:, b, :].bitcast(F32)
+        def turn_bank(load, bank):
+            part, block = divmod(load, ROW_BLOCKS)
+            half, b = divmod(block, HALF_BLOCKS)
+            words = x_raw[load][:].bitcast(F32)
+            turned = turns.tile([P, BANK_PASSES, PAIRS, P], F32, tag="turned")
+            for g in range(BANK_PASSES):
+                first = (bank * BANK_PASSES + g) * PASS_WORDS
+                for u in range(PAIRS):
                     nc.tensor.transpose(
-                        turned[:, u, b * P : (b + 1) * P],
-                        words[:, g * PASS_WORDS + u : (g + 1) * PASS_WORDS : PAIRS],
-                        ident[:],
+                        turned[:, g, u, :], words[:, first + u : first + PASS_WORDS : PAIRS], ident[:]
                     )
-            x_grouped[bank] = x_stage.tile([P, BANK_ROWS * PACK], BF16, align_bytes=64, name="x_grouped")
-            grouped_words = x_grouped[bank][:].bitcast(F32).rearrange("p (n u) -> p n u", u=PAIRS)
-            planes_alternately = turned[:].rearrange("p u n -> p n u")
-            if bank % VECTOR_EVERY == VECTOR_EVERY - 1:
+            first_pass = part * X_LOAD_PASSES + bank * BANK_PASSES
+            if b == 0:
+                x_grouped[first_pass, half] = x_stage.tile(
+                    [P, BANK_PASSES, HALF_ROWS * PACK], BF16, align_bytes=64, name="x_grouped"
+                )
+            grouped_words = (
+                x_grouped[first_pass, half][:, :, b * P * PACK : (b + 1) * P * PACK]
+                .bitcast(F32)
+                .rearrange("p g (n u) -> p g n u", u=PAIRS)
+            )
+            planes_alternately = turned[:].rearrange("p g u n -> p g n u")
+            if b == 0 and bank % 2 == 1:
                 nc.vector.tensor_copy(out=grouped_words, in_=planes_alternately)
             else:
                 nc.scalar.copy(out=grouped_words, in_=planes_alternately)
 
-        def quantise_bank(bank):
-            load, g = divmod(bank, X_LOAD_PASSES)
-            part, half = divmod(load, ROW_HALVES)
-            sentences = slice(half * BANK_ROWS, (half + 1) * BANK_ROWS)
-            nc.vector.quantize_mx(
-                out=x_codes[:, part * X_LOAD_PASSES + g, sentences].bitcast(FP8X4),
-                scales=x_scales[:, part * X_LOAD_PASSES + g, sentences],
-                in_=x_grouped[bank][:],
-            )
+        def quantise_bank(first_pass, half):
+            sentences = slice(half * HALF_ROWS, (half + 1) * HALF_ROWS)
+            for g in range(BANK_PASSES):
+                nc.vector.quantize_mx(
+                    out=x_codes[:, first_pass + g, sentences].bitcast(FP8X4),
+                    scales=x_scales[:, first_pass + g, sentences],
+                    in_=x_grouped[first_pass, half][:, g, :],
+                )
 
         def load_w(piece):
-            part, tap = divmod(piece, TAPS)
-            w_raw[piece] = w_loads.tile([P, PIECE_PASSES, PACK * C], BF16, name="w_raw")
+            tap, first_pass, passes = PIECES[piece]
+            w_raw[piece] = w_loads.tile([P, passes, PACK * C], BF16, name="w_raw")
             nc.sync.dma_start(
                 out=w_raw[piece][:],
-                in_=W1[tap, part * PIECE_K : (part + 1) * PIECE_K, :].rearrange(
+                in_=W1[tap, first_pass * K_PASS : (first_pass + passes) * K_PASS, :].rearrange(
                     "(g p j) c -> p g (j c)", p=P, j=PACK
                 ),
             )
 
         def regroup_w(piece):
-            w_grouped[piece] = w_stage.tile(
-                [P, PIECE_PASSES, C * PACK], BF16, align_bytes=64, name="w_grouped"
-            )
+            passes = PIECES[piece][2]
+            w_grouped[piece] = w_stage.tile([P, passes, C * PACK], BF16, align_bytes=64, name="w_grouped")
             side_by_side = w_grouped[piece][:].rearrange("p g (c i j) -> p g c j i", i=RUN, j=PACK)
             rows_apart = w_raw[piece][:].rearrange("p g (j c i) -> p g c j i", j=PACK, i=RUN)
             nc.vector.tensor_copy(
-                out=side_by_side[:, 0:VECTOR_PASSES], in_=rows_apart[:, 0:VECTOR_PASSES]
+                out=side_by_side[:, 0 : passes // 2], in_=rows_apart[:, 0 : passes // 2]
             )
-            for g in range(VECTOR_PASSES, PIECE_PASSES):
+            for g in range(passes // 2, passes):
                 nc.scalar.copy(out=side_by_side[:, g], in_=rows_apart[:, g])
 
         def quantise_w(piece):
-            w_codes[piece] = w_stage.tile([P, PIECE_PASSES * C], U32, align_bytes=64, name="w_codes")
-            w_scales[piece] = w_stage.tile([P, PIECE_PASSES * C], U8, align_bytes=64, name="w_scales")
+            passes = PIECES[piece][2]
+            w_codes[piece] = w_quantised.tile([P, passes * C], U32, align_bytes=64, name="w_codes")
+            w_scales[piece] = w_quantised.tile([P, passes * C], U8, align_bytes=64, name="w_scales")
             nc.vector.quantize_mx(
                 out=w_codes[piece][:].bitcast(FP8X4),
                 scales=w_scales[piece][:],
@@ -149,40 +161,55 @@ def tile_predictor_pa_k_kernel(tc, x, W1, b1, out):
             )
 
         def multiply(piece):
-            part, tap = divmod(piece, TAPS)
-            for g in range(PIECE_PASSES):
-                pass_index = part * PIECE_PASSES + g
+            tap, first_pass, passes = PIECES[piece]
+            for g in range(passes):
                 channels = slice(g * C, (g + 1) * C)
                 nc.tensor.matmul_mx(
                     out=acc[tap][:],
                     lhsT=w_codes[piece][:, channels].bitcast(FP8X4),
                     lhsT_scale=w_scales[piece][:, channels],
-                    rhs=x_codes[:, pass_index, :].bitcast(FP8X4),
-                    rhs_scale=x_scales[:, pass_index, :],
-                    start=(pass_index == 0),
-                    stop=(pass_index == PASSES - 1),
+                    rhs=x_codes[:, first_pass + g, :].bitcast(FP8X4),
+                    rhs_scale=x_scales[:, first_pass + g, :],
+                    start=(first_pass + g == 0),
+                    stop=(first_pass + g == PASSES - 1),
                 )
 
         with tc.manual_schedule():
+            for piece in range(HEAD_PIECES):
+                load_w(piece)
             for load in range(X_BUFS):
                 load_x(load)
-            for bank in range(X_BANKS + 1):
-                if bank < X_BANKS:
-                    turn_bank(bank)
-                    next_load = bank // X_LOAD_PASSES + X_BUFS
-                    if bank % X_LOAD_PASSES == X_LOAD_PASSES - 1 and next_load < X_LOADS:
-                        load_x(next_load)
-                if bank > 0:
-                    quantise_bank(bank - 1)
+            for piece in range(HEAD_PIECES):
+                regroup_w(piece)
+            for piece in range(HEAD_PIECES):
+                quantise_w(piece)
 
-            for piece in range(W_BUFS):
+            ready = []
+            for load in range(X_LOADS):
+                part, block = divmod(load, ROW_BLOCKS)
+                half, b = divmod(block, HALF_BLOCKS)
+                for bank in range(X_LOAD_BANKS):
+                    turn_bank(load, bank)
+                    for filled in ready:
+                        quantise_bank(*filled)
+                    ready = []
+                    if b == HALF_BLOCKS - 1:
+                        ready = [(part * X_LOAD_PASSES + bank * BANK_PASSES, half)]
+                if load + X_BUFS < X_LOADS:
+                    load_x(load + X_BUFS)
+            for filled in ready:
+                quantise_bank(*filled)
+
+            for piece in range(HEAD_PIECES, HEAD_PIECES + W_BUFS):
                 load_w(piece)
-            for piece in range(PIECES + 1):
-                if piece < PIECES:
+            for piece in range(HEAD_PIECES):
+                multiply(piece)
+            for piece in range(HEAD_PIECES, len(PIECES) + 1):
+                if piece < len(PIECES):
                     regroup_w(piece)
-                    if piece + W_BUFS < PIECES:
+                    if piece + W_BUFS < len(PIECES):
                         load_w(piece + W_BUFS)
-                if piece > 0:
+                if piece > HEAD_PIECES:
                     quantise_w(piece - 1)
                     multiply(piece - 1)
 
@@ -190,21 +217,27 @@ def tile_predictor_pa_k_kernel(tc, x, W1, b1, out):
             nc.vector.tensor_scalar(
                 out=shifted[:], in0=acc[0][:], scalar1=bias[:, 0:1], scalar2=None, op0=ALU.add
             )
-            for tap in range(1, TAPS):
+            def add_tap(tap, begin, end):
+                begin = max(begin, tap)
                 nc.vector.scalar_tensor_tensor(
-                    out=shifted[:, tap:ROWS],
-                    in0=acc[tap][:, 0 : ROWS - tap],
+                    out=shifted[:, begin:end],
+                    in0=acc[tap][:, begin - tap : end - tap],
                     scalar=bias[:, 0:1],
-                    in1=shifted[:, tap:ROWS],
+                    in1=shifted[:, begin:end],
                     op0=ALU.add,
                     op1=ALU.add,
                 )
 
-            result_turned = turns.tile([P, ROW_BLOCKS, C], F32, tag="turned")
-            for r in range(ROW_BLOCKS):
-                nc.tensor.transpose(
-                    result_turned[:, r, :], shifted[:, r * P : (r + 1) * P], ident[:]
-                )
-            result = consts.tile([P, ROW_BLOCKS, C], F32)
-            nc.scalar.activation(out=result[:], in_=result_turned[:], func=ACT.Tanh)
-            nc.sync.dma_start(out=out.rearrange("(r p) c -> p r c", p=P), in_=result[:])
+            for tap in range(1, TAPS - 1):
+                add_tap(tap, 0, ROWS)
+
+            out_by_half = out.rearrange("(h r p) c -> h p r c", r=HALF_BLOCKS, p=P)
+            for half in range(ROW_BLOCKS // HALF_BLOCKS):
+                add_tap(TAPS - 1, half * HALF_ROWS, (half + 1) * HALF_ROWS)
+                result_turned = turns.tile([P, HALF_BLOCKS, C], F32, tag="turned")
+                for b in range(HALF_BLOCKS):
+                    begin = half * HALF_ROWS + b * P
+                    nc.tensor.transpose(result_turned[:, b, :], shifted[:, begin : begin + P], ident[:])
+                result = x_stage.tile([P, HALF_BLOCKS, C], F32, name="result")
+                nc.scalar.activation(out=result[:], in_=result_turned[:], func=ACT.Tanh)
+                nc.sync.dma_start(out=out_by_half[half], in_=result[:])

@@ -44,7 +44,7 @@ PIECES = WHOLE_PIECES[:-1] + [
 ]
 W_BUFS = 8
 HEAD_PIECES = 2
-RUN = 4
+RUN = 8
 
 FLOPS = 2 * ROWS * K * C * TAPS
 

@@ -33,17 +33,22 @@ X_BUFS = 8
 HALF_BLOCKS = 2
 HALF_ROWS = HALF_BLOCKS * P
 
-PART_PASSES = 4
-SHORT_PASSES = PART_PASSES // 2
-WHOLE_PIECES = [
-    (tap, part * PART_PASSES, PART_PASSES) for part in range(PASSES // PART_PASSES) for tap in range(TAPS)
+LOAD_PASSES = 4
+HALF_PASSES = LOAD_PASSES // 2
+FINE_FROM = PASSES - 2 * LOAD_PASSES
+W_LOADS = [
+    (tap, first_pass, LOAD_PASSES) for first_pass in range(0, PASSES, LOAD_PASSES) for tap in range(TAPS)
+][:-1] + [
+    (TAPS - 1, first_pass, HALF_PASSES) for first_pass in range(PASSES - LOAD_PASSES, PASSES, HALF_PASSES)
 ]
-PIECES = WHOLE_PIECES[:-1] + [
-    (TAPS - 1, PASSES - 2 * SHORT_PASSES, SHORT_PASSES),
-    (TAPS - 1, PASSES - SHORT_PASSES, SHORT_PASSES),
+PIECES = [
+    (load, begin, min(passes, HALF_PASSES if first_pass >= FINE_FROM else LOAD_PASSES))
+    for load, (tap, first_pass, passes) in enumerate(W_LOADS)
+    for begin in range(0, passes, HALF_PASSES if first_pass >= FINE_FROM else LOAD_PASSES)
 ]
 W_BUFS = 8
-HEAD_PIECES = 2
+HEAD_LOADS = 2
+HEAD_PIECES = HEAD_LOADS
 RUN = 8
 
 FLOPS = 2 * ROWS * K * C * TAPS
@@ -83,7 +88,8 @@ def tile_predictor_pa_k_kernel(tc, x, W1, b1, out):
         acc = [sums.tile([P, ROWS], F32, name="acc%d" % tap) for tap in range(TAPS)]
         x_raw = {}
         x_grouped = {}
-        w_raw, w_grouped, w_codes, w_scales = {}, {}, {}, {}
+        w_raw = {}
+        w_grouped, w_codes, w_scales = {}, {}, {}
 
         def load_x(load):
             part, block = divmod(load, ROW_BLOCKS)
@@ -129,21 +135,22 @@ def tile_predictor_pa_k_kernel(tc, x, W1, b1, out):
                     in_=x_grouped[first_pass, half][:, g, :],
                 )
 
-        def load_w(piece):
-            tap, first_pass, passes = PIECES[piece]
-            w_raw[piece] = w_loads.tile([P, passes, PACK * C], BF16, name="w_raw")
+        def load_w(load):
+            tap, first_pass, passes = W_LOADS[load]
+            w_raw[load] = w_loads.tile([P, passes, PACK * C], BF16, name="w_raw")
             nc.sync.dma_start(
-                out=w_raw[piece][:],
+                out=w_raw[load][:],
                 in_=W1[tap, first_pass * K_PASS : (first_pass + passes) * K_PASS, :].rearrange(
                     "(g p j) c -> p g (j c)", p=P, j=PACK
                 ),
             )
 
         def regroup_w(piece):
-            passes = PIECES[piece][2]
+            load, begin, passes = PIECES[piece]
             w_grouped[piece] = w_stage.tile([P, passes, C * PACK], BF16, align_bytes=64, name="w_grouped")
             side_by_side = w_grouped[piece][:].rearrange("p g (c i j) -> p g c j i", i=RUN, j=PACK)
-            rows_apart = w_raw[piece][:].rearrange("p g (j c i) -> p g c j i", j=PACK, i=RUN)
+            raw = w_raw[load][:, begin : begin + passes, :]
+            rows_apart = raw.rearrange("p g (j c i) -> p g c j i", j=PACK, i=RUN)
             nc.vector.tensor_copy(
                 out=side_by_side[:, 0 : passes // 2], in_=rows_apart[:, 0 : passes // 2]
             )
@@ -161,7 +168,9 @@ def tile_predictor_pa_k_kernel(tc, x, W1, b1, out):
             )
 
         def multiply(piece):
-            tap, first_pass, passes = PIECES[piece]
+            load, begin, passes = PIECES[piece]
+            tap = W_LOADS[load][0]
+            first_pass = W_LOADS[load][1] + begin
             for g in range(passes):
                 channels = slice(g * C, (g + 1) * C)
                 nc.tensor.matmul_mx(
@@ -175,8 +184,8 @@ def tile_predictor_pa_k_kernel(tc, x, W1, b1, out):
                 )
 
         with tc.manual_schedule():
-            for piece in range(HEAD_PIECES):
-                load_w(piece)
+            for load in range(HEAD_LOADS):
+                load_w(load)
             for load in range(X_BUFS):
                 load_x(load)
             for piece in range(HEAD_PIECES):
@@ -200,22 +209,23 @@ def tile_predictor_pa_k_kernel(tc, x, W1, b1, out):
             for filled in ready:
                 quantise_bank(*filled)
 
-            for piece in range(HEAD_PIECES, HEAD_PIECES + W_BUFS):
-                load_w(piece)
+            for load in range(HEAD_LOADS, HEAD_LOADS + W_BUFS):
+                load_w(load)
             for piece in range(HEAD_PIECES):
                 multiply(piece)
             for piece in range(HEAD_PIECES, len(PIECES) + 1):
                 if piece < len(PIECES):
                     regroup_w(piece)
-                    if piece + W_BUFS < len(PIECES):
-                        load_w(piece + W_BUFS)
+                    load, begin, passes = PIECES[piece]
+                    if begin + passes == W_LOADS[load][2] and load + W_BUFS < len(W_LOADS):
+                        load_w(load + W_BUFS)
                 if piece > HEAD_PIECES:
                     quantise_w(piece - 1)
                     multiply(piece - 1)
 
             shifted = consts.tile([P, ROWS], F32)
-            nc.vector.tensor_scalar(
-                out=shifted[:], in0=acc[0][:], scalar1=bias[:, 0:1], scalar2=None, op0=ALU.add
+            nc.scalar.activation(
+                out=shifted[:], in_=acc[0][:], func=ACT.Identity, bias=bias[:, 0:1]
             )
             def add_tap(tap, begin, end):
                 begin = max(begin, tap)

from contextlib import ExitStack

import concourse.mybir as mybir
from concourse.masks import make_identity

FP8X4 = mybir.dt.float8_e4m3fn_x4
BF16 = mybir.dt.bfloat16
F32 = mybir.dt.float32
U32 = mybir.dt.uint32
U8 = mybir.dt.uint8
ACT = mybir.ActivationFunctionType
ALU = mybir.AluOpType

P = 128
PACK = 4
K_PASS = P * PACK
PAIRS = PACK // 2
PASS_WORDS = K_PASS // 2

ROWS = 512
K = 16384
C = 128
TAPS = 3
ROW_BLOCKS = ROWS // P
PASSES = K // K_PASS

BANK_PASSES = 2
X_LOAD_PASSES = 8
X_LOAD_K = X_LOAD_PASSES * K_PASS
X_LOAD_BANKS = X_LOAD_PASSES // BANK_PASSES
X_LOADS = ROW_BLOCKS * K // X_LOAD_K
X_BUFS = 8
HALF_BLOCKS = 2
HALF_ROWS = HALF_BLOCKS * P

LOAD_PASSES = 4
HALF_PASSES = LOAD_PASSES // 2
FINE_FROM = PASSES - 2 * LOAD_PASSES
W_LOADS = [
    (tap, first_pass, LOAD_PASSES) for first_pass in range(0, PASSES, LOAD_PASSES) for tap in range(TAPS)
][:-1] + [
    (TAPS - 1, first_pass, HALF_PASSES) for first_pass in range(PASSES - LOAD_PASSES, PASSES, HALF_PASSES)
]
PIECES = [
    (load, begin, min(passes, HALF_PASSES if first_pass >= FINE_FROM else LOAD_PASSES))
    for load, (tap, first_pass, passes) in enumerate(W_LOADS)
    for begin in range(0, passes, HALF_PASSES if first_pass >= FINE_FROM else LOAD_PASSES)
]
W_BUFS = 8
HEAD_LOADS = 2
HEAD_PIECES = HEAD_LOADS
RUN = 8

FLOPS = 2 * ROWS * K * C * TAPS


def tile_predictor_pa_k_kernel(tc, x, W1, b1, out):
    nc = tc.nc
    with ExitStack() as pools:
        consts = pools.enter_context(tc.tile_pool(name="consts", bufs=1))
        x_loads = pools.enter_context(tc.tile_pool(name="x_loads", bufs=X_BUFS))
        x_stage = pools.enter_context(tc.tile_pool(name="x_stage", bufs=7))
        w_loads = pools.enter_context(tc.tile_pool(name="w_loads", bufs=W_BUFS))
        w_stage = pools.enter_context(tc.tile_pool(name="w_stage", bufs=3))
        w_quantised = pools.enter_context(tc.tile_pool(name="w_quantised", bufs=HEAD_PIECES + 2))
        sums = pools.enter_context(tc.psum_pool(name="sums", bufs=1))
        turns = pools.enter_context(tc.psum_pool(name="turns", bufs=5))

        ident = consts.tile([P, P], F32)
        make_identity(nc, ident[:])

        warm = consts.tile([P, 1], F32)
        nc.vector.memset(warm[:], 0.0)
        nc.scalar.activation(out=warm[:], in_=warm[:], func=ACT.Tanh)

        bias_row = consts.tile([1, C], BF16)
        nc.sync.dma_start(out=bias_row[:], in_=b1)
        bias_rows = consts.tile([P, P], F32)
        nc.vector.memset(bias_rows[:], 0.0)
        nc.vector.tensor_copy(out=bias_rows[0:1, :], in_=bias_row[:])
        bias_turned = turns.tile([P, P], F32, tag="turned")
        nc.tensor.transpose(bias_turned[:], bias_rows[:], ident[:])
        bias = consts.tile([P, 1], F32)
        nc.vector.tensor_copy(out=bias[:], in_=bias_turned[:, 0:1])

        x_codes = consts.tile([P, PASSES, ROWS], U32, align_bytes=64)
        x_scales = consts.tile([P, PASSES, ROWS], U8, align_bytes=64)
        acc = [sums.tile([P, ROWS], F32, name="acc%d" % tap) for tap in range(TAPS)]
        x_raw = {}
        x_grouped = {}
        w_raw = {}
        w_grouped, w_codes, w_scales = {}, {}, {}

        def load_x(load):
            part, block = divmod(load, ROW_BLOCKS)
            x_raw[load] = x_loads.tile([P, X_LOAD_K], BF16, name="x_raw")
            nc.sync.dma_start(
                out=x_raw[load][:],
                in_=x[block * P : (block + 1) * P, part * X_LOAD_K : (part + 1) * X_LOAD_K],
            )

        def turn_bank(load, bank):
            part, block = divmod(load, ROW_BLOCKS)
            half, b = divmod(block, HALF_BLOCKS)
            words = x_raw[load][:].bitcast(F32)
            turned = turns.tile([P, BANK_PASSES, PAIRS, P], F32, tag="turned")
            for g in range(BANK_PASSES):
                first = (bank * BANK_PASSES + g) * PASS_WORDS
                for u in range(PAIRS):
                    nc.tensor.transpose(
                        turned[:, g, u, :], words[:, first + u : first + PASS_WORDS : PAIRS], ident[:]
                    )
            first_pass = part * X_LOAD_PASSES + bank * BANK_PASSES
            if b == 0:
                x_grouped[first_pass, half] = x_stage.tile(
                    [P, BANK_PASSES, HALF_ROWS * PACK], BF16, align_bytes=64, name="x_grouped"
                )
            grouped_words = (
                x_grouped[first_pass, half][:, :, b * P * PACK : (b + 1) * P * PACK]
                .bitcast(F32)
                .rearrange("p g (n u) -> p g n u", u=PAIRS)
            )
            planes_alternately = turned[:].rearrange("p g u n -> p g n u")
            if b == 0 and bank % 2 == 1:
                nc.vector.tensor_copy(out=grouped_words, in_=planes_alternately)
            else:
                nc.scalar.copy(out=grouped_words, in_=planes_alternately)

        def quantise_bank(first_pass, half):
            sentences = slice(half * HALF_ROWS, (half + 1) * HALF_ROWS)
            for g in range(BANK_PASSES):
                nc.vector.quantize_mx(
                    out=x_codes[:, first_pass + g, sentences].bitcast(FP8X4),
                    scales=x_scales[:, first_pass + g, sentences],
                    in_=x_grouped[first_pass, half][:, g, :],
                )

        def load_w(load):
            tap, first_pass, passes = W_LOADS[load]
            w_raw[load] = w_loads.tile([P, passes, PACK * C], BF16, name="w_raw")
            nc.sync.dma_start(
                out=w_raw[load][:],
                in_=W1[tap, first_pass * K_PASS : (first_pass + passes) * K_PASS, :].rearrange(
                    "(g p j) c -> p g (j c)", p=P, j=PACK
                ),
            )

        def regroup_w(piece):
            load, begin, passes = PIECES[piece]
            w_grouped[piece] = w_stage.tile([P, passes, C * PACK], BF16, align_bytes=64, name="w_grouped")
            side_by_side = w_grouped[piece][:].rearrange("p g (c i j) -> p g c j i", i=RUN, j=PACK)
            raw = w_raw[load][:, begin : begin + passes, :]
            rows_apart = raw.rearrange("p g (j c i) -> p g c j i", j=PACK, i=RUN)
            nc.vector.tensor_copy(
                out=side_by_side[:, 0 : passes // 2], in_=rows_apart[:, 0 : passes // 2]
            )
            for g in range(passes // 2, passes):
                nc.scalar.copy(out=side_by_side[:, g], in_=rows_apart[:, g])

        def quantise_w(piece):
            passes = PIECES[piece][2]
            w_codes[piece] = w_quantised.tile([P, passes * C], U32, align_bytes=64, name="w_codes")
            w_scales[piece] = w_quantised.tile([P, passes * C], U8, align_bytes=64, name="w_scales")
            nc.vector.quantize_mx(
                out=w_codes[piece][:].bitcast(FP8X4),
                scales=w_scales[piece][:],
                in_=w_grouped[piece][:].rearrange("p g f -> p (g f)"),
            )

        def multiply(piece):
            load, begin, passes = PIECES[piece]
            tap = W_LOADS[load][0]
            first_pass = W_LOADS[load][1] + begin
            for g in range(passes):
                channels = slice(g * C, (g + 1) * C)
                nc.tensor.matmul_mx(
                    out=acc[tap][:],
                    lhsT=w_codes[piece][:, channels].bitcast(FP8X4),
                    lhsT_scale=w_scales[piece][:, channels],
                    rhs=x_codes[:, first_pass + g, :].bitcast(FP8X4),
                    rhs_scale=x_scales[:, first_pass + g, :],
                    start=(first_pass + g == 0),
                    stop=(first_pass + g == PASSES - 1),
                )

        with tc.manual_schedule():
            for load in range(HEAD_LOADS):
                load_w(load)
            for load in range(X_BUFS):
                load_x(load)
            for piece in range(HEAD_PIECES):
                regroup_w(piece)
            for piece in range(HEAD_PIECES):
                quantise_w(piece)

            ready = []
            for load in range(X_LOADS):
                part, block = divmod(load, ROW_BLOCKS)
                half, b = divmod(block, HALF_BLOCKS)
                for bank in range(X_LOAD_BANKS):
                    turn_bank(load, bank)
                    for filled in ready:
                        quantise_bank(*filled)
                    ready = []
                    if b == HALF_BLOCKS - 1:
                        ready = [(part * X_LOAD_PASSES + bank * BANK_PASSES, half)]
                if load + X_BUFS < X_LOADS:
                    load_x(load + X_BUFS)
            for filled in ready:
                quantise_bank(*filled)

            for load in range(HEAD_LOADS, HEAD_LOADS + W_BUFS):
                load_w(load)
            for piece in range(HEAD_PIECES):
                multiply(piece)
            for piece in range(HEAD_PIECES, len(PIECES) + 1):
                if piece < len(PIECES):
                    regroup_w(piece)
                    load, begin, passes = PIECES[piece]
                    if begin + passes == W_LOADS[load][2] and load + W_BUFS < len(W_LOADS):
                        load_w(load + W_BUFS)
                if piece > HEAD_PIECES:
                    quantise_w(piece - 1)
                    multiply(piece - 1)

            shifted = consts.tile([P, ROWS], F32)
            nc.scalar.activation(
                out=shifted[:], in_=acc[0][:], func=ACT.Identity, bias=bias[:, 0:1]
            )
            def add_tap(tap, begin, end):
                begin = max(begin, tap)
                nc.vector.scalar_tensor_tensor(
                    out=shifted[:, begin:end],
                    in0=acc[tap][:, begin - tap : end - tap],
                    scalar=bias[:, 0:1],
                    in1=shifted[:, begin:end],
                    op0=ALU.add,
                    op1=ALU.add,
                )

            for tap in range(1, TAPS - 1):
                add_tap(tap, 0, ROWS)

            out_by_half = out.rearrange("(h r p) c -> h p r c", r=HALF_BLOCKS, p=P)
            for half in range(ROW_BLOCKS // HALF_BLOCKS):
                add_tap(TAPS - 1, half * HALF_ROWS, (half + 1) * HALF_ROWS)
                result_turned = turns.tile([P, HALF_BLOCKS, C], F32, tag="turned")
                for b in range(HALF_BLOCKS):
                    begin = half * HALF_ROWS + b * P
                    nc.tensor.transpose(result_turned[:, b, :], shifted[:, begin : begin + P], ident[:])
                result = x_stage.tile([P, HALF_BLOCKS, C], F32, name="result")
                nc.scalar.activation(out=result[:], in_=result_turned[:], func=ACT.Tanh)
                nc.sync.dma_start(out=out_by_half[half], in_=result[:])
